import numpy as np
import ml_dtypes


def mxq(x, axis, fmt="e4m3"):
    dtype, down = {"e4m3": (ml_dtypes.float8_e4m3fn, 7), "e5m2": (ml_dtypes.float8_e5m2, 14)}[fmt]
    v = np.moveaxis(np.asarray(x, np.float32).astype(ml_dtypes.bfloat16).astype(np.float64), axis, -1)
    blocks = v.reshape(v.shape[:-1] + (-1, 32))
    amax = np.abs(blocks).max(-1, keepdims=True)
    byte = np.maximum(np.where(amax > 0, np.frexp(amax)[1] - 1 + 127, 0) - down, 1)
    scale = np.exp2(byte - 127.0)
    codes = (blocks / scale).astype(np.float32).astype(dtype).astype(np.float64)
    return np.moveaxis((codes * scale).reshape(v.shape), -1, axis)


WIDE = False


def mx_kscale(k):
    if not WIDE:
        return np.ones(k)
    levels = np.array([10, -10, 5, -5, 0])
    if k % 512:
        return np.exp2(np.random.permutation(np.resize(levels, k // 32))).repeat(32)
    a = np.empty((k // 512, 16))
    for p in range(k // 512):
        a[p, :8] = np.random.permutation(np.resize(levels, 8))
        for g in range(8):
            far = levels[np.abs(levels - a[p, g]) >= 10]
            a[p, g + 8] = far[np.random.randint(len(far))]
    return np.exp2(a.ravel()).repeat(32)


BF16 = ml_dtypes.bfloat16


def bf(x):
    return np.asarray(x, np.float32).astype(BF16)


def f64(x):
    return np.asarray(x).astype(np.float64)


B, K, N = 16384, 512, 256


def draw0():
    s = mx_kscale(K)
    return {"x": bf(np.random.standard_normal((B, K)) * s),
            "dft_real": bf(np.random.standard_normal((N, K)) / np.sqrt(K) / s[None, :]),
            "dft_imag": bf(np.random.standard_normal((N, K)) / np.sqrt(K) / s[None, :])}


def core(x, dft_real, dft_imag):
    xq = mxq(f64(x), 1, "e4m3")
    rxs = xq @ mxq(f64(dft_real), 1, "e4m3").T
    ixs = xq @ mxq(f64(dft_imag), 1, "e4m3").T
    mag = np.log(rxs * rxs + ixs * ixs)
    return mag


def e4m3fn_bytes(y):
    return np.clip(np.asarray(y, np.float64), -448.0, 448.0).astype(np.float32).astype(ml_dtypes.float8_e4m3fn).view(np.uint8)


def e4m3fn_values(b):
    return np.asarray(b, np.uint8).view(ml_dtypes.float8_e4m3fn).astype(np.float64)


def setup_inputs():
    d = draw0()
    x0 = np.asarray(d['x']).astype(np.float64)
    s = (np.max(np.abs(x0), axis=(0,), keepdims=True) / 448.0).astype(np.float32)
    out = {}
    for k, v in d.items():
        if k == 'x':
            out['x_bytes'] = e4m3fn_bytes(x0 / s.astype(np.float64))
            out['x_scale'] = s
        else:
            out[k] = v
    return out


def reference(x_bytes, x_scale, dft_real, dft_imag):
    return core(e4m3fn_values(x_bytes) * x_scale.astype(np.float64), dft_real, dft_imag)

@@ -1,0 +1,311 @@
+from contextlib import ExitStack
+
+import concourse.mybir as mybir
+from concourse.masks import make_identity
+
+B, K, N = 16384, 512, 256
+FLOPS = 2 * B * K * 2 * N
+
+F32 = mybir.dt.float32
+BF16 = mybir.dt.bfloat16
+U32 = mybir.dt.uint32
+U8 = mybir.dt.uint8
+FP8 = mybir.dt.float8_e4m3fn
+FP8X4 = mybir.dt.float8_e4m3fn_x4
+ACT = mybir.ActivationFunctionType
+ALU = mybir.AluOpType
+
+P = 128
+SUB = 4
+NCH = B // (P * SUB)
+W2 = 2 * N
+PERM = False
+
+
+HEAD = [[2, 2], [2, 2]]
+TAIL = [[2, 2]]
+
+
+def unit_list():
+    sizes = HEAD + [[4]] * (NCH - len(HEAD) - len(TAIL)) + TAIL
+    units = []
+    for c, parts in enumerate(sizes):
+        j0 = 0
+        for nj in parts:
+            units.append((c, j0, nj))
+            j0 += nj
+    return units
+
+
+def is_half(i, nj):
+    return nj == 4 and i % 3 == 1
+
+
+def copy_on_vector(i, h, nu):
+    if i >= nu - 4:
+        return True
+    if i < 6:
+        return False
+    return i % 3 != 0
+
+
+def permuted(ap):
+    return ap.rearrange("p (w g i) -> p g w i", w=2, i=16)
+
+
+def plain(ap):
+    return ap.rearrange("p (g w i) -> p g w i", w=2, i=16)
+
+
+def tile_dft_kernel(tc, x_bytes, x_scale, dft_real, dft_imag, out):
+    nc = tc.nc
+    units = unit_list()
+    nu = len(units)
+    xv = x_bytes.rearrange("(c p j) k -> c p j k", p=P, j=SUB)
+    ov = out.rearrange("(c p j) n -> c p j n", p=P, j=SUB)
+
+    with ExitStack() as ctx:
+        const = ctx.enter_context(tc.tile_pool(name="const", bufs=1))
+        bpool = ctx.enter_context(tc.tile_pool(name="bpool", bufs=NCH))
+        work = ctx.enter_context(tc.tile_pool(name="work", bufs=3))
+        outp = ctx.enter_context(tc.tile_pool(name="outp", bufs=8))
+        px = ctx.enter_context(tc.psum_pool(name="px", bufs=2))
+        pm = ctx.enter_context(tc.psum_pool(name="pm", bufs=4))
+        po = ctx.enter_context(tc.psum_pool(name="po", bufs=2))
+        ctx.enter_context(tc.manual_schedule())
+
+        sc = const.tile([P, SUB * K], F32, name="sc")
+        nc.sync.dma_start(out=sc[:, 0:K], in_=x_scale.rearrange("o k -> (o k)").partition_broadcast(P))
+
+        wr = const.tile([P, 4 * K], BF16, name="wr")
+        xb = []
+        for c in range(NCH):
+            xbytes = bpool.tile([P, SUB * K], U8, name="xbytes", tag="xbytes")
+            nc.sync.dma_start(out=xbytes[:].rearrange("p (j k) -> p j k", j=SUB), in_=xv[c])
+            xb.append(xbytes)
+            if c == 0:
+                nc.sync.dma_start(
+                    out=wr[:, 0 : 2 * K].rearrange("p (b k) -> p b k", b=2),
+                    in_=dft_real.rearrange("(b p) k -> p b k", p=P),
+                )
+                nc.sync.dma_start(
+                    out=wr[:, 2 * K : 4 * K].rearrange("p (b k) -> p b k", b=2),
+                    in_=dft_imag.rearrange("(b p) k -> p b k", p=P),
+                )
+
+        ident = const.tile([P, P], F32, name="ident")
+        make_identity(nc, ident[:])
+        one = const.tile([P, 1], F32, name="one")
+        nc.vector.memset(one[:], 1.0)
+        warm = const.tile([P, 1], F32, name="warm")
+        nc.scalar.activation(out=warm[:], in_=one[:], func=ACT.Ln)
+        if PERM:
+            wp = const.tile([P, 4 * K], BF16, name="wp")
+            for half in range(2):
+                nc.scalar.copy(
+                    out=permuted(wp[:])[:, half * 32 : (half + 1) * 32, :, :],
+                    in_=plain(wr[:])[:, half * 32 : (half + 1) * 32, :, :],
+                )
+        else:
+            wp = wr
+        nc.scalar.copy(out=sc[:, K : 2 * K], in_=sc[:, 0:K])
+        nc.scalar.copy(out=sc[:, 2 * K : 4 * K], in_=sc[:, 0 : 2 * K])
+
+        wc = const.tile([P, W2], U32, name="wc", align_bytes=64)
+        wsc = const.tile([P, W2], U8, name="wsc", align_bytes=64)
+
+        st = {}
+
+        def transposes(key, src, nj):
+            words = src.bitcast(F32)
+            banks = []
+            for h in range((nj + 1) // 2):
+                xt = px.tile([P, 2, 2, P], F32, name="xt", tag="xt")
+                for jj in range(min(2, nj - 2 * h)):
+                    j = 2 * h + jj
+                    for w in range(2):
+                        if PERM:
+                            cols = words[:, (w * nj + j) * P : (w * nj + j + 1) * P]
+                        else:
+                            cols = words[:, 256 * j + w : 256 * (j + 1) : 2]
+                        nc.tensor.transpose(xt[:, jj, w, :], cols, ident[:])
+                banks.append(xt)
+            st[("xt", key)] = banks
+
+        def copy_out(key, nj, on_vector):
+            gx = work.tile([P, nj * 4 * P], BF16, name="gx", tag="gx", align_bytes=64)
+            gw = gx[:].bitcast(F32)
+            for h, xt in enumerate(st[("xt", key)]):
+                njj = min(2, nj - 2 * h)
+                dst = gw[:, 512 * h : 512 * h + 256 * njj].rearrange("p (j r w) -> p j r w", j=njj, w=2)
+                src = xt[:, 0:njj, :, :].rearrange("p j w r -> p j r w")
+                if on_vector(h):
+                    nc.vector.tensor_copy(out=dst, in_=src)
+                else:
+                    nc.scalar.copy(out=dst, in_=src)
+            st[("gx", key)] = gx
+
+        def quantize(key, codes, scales):
+            nc.vector.quantize_mx(out=codes.bitcast(FP8X4), scales=scales, in_=st[("gx", key)][:])
+
+        def stage_p(i):
+            c, j0, nj = units[i]
+            xs = work.tile([P, nj * K], BF16, name="xs", tag="xs")
+            if PERM:
+                nc.vector.tensor_tensor(
+                    out=permuted(xs[:]),
+                    in0=plain(xb[c][:, j0 * K : (j0 + nj) * K].bitcast(FP8)),
+                    in1=plain(sc[:, 0 : nj * K]),
+                    op=ALU.mult,
+                )
+            elif c == 0:
+                for j in range(nj):
+                    nc.vector.tensor_tensor(
+                        out=xs[:, j * K : (j + 1) * K],
+                        in0=xb[c][:, (j0 + j) * K : (j0 + j + 1) * K].bitcast(FP8),
+                        in1=sc[:, 0:K],
+                        op=ALU.mult,
+                    )
+            else:
+                nc.vector.tensor_tensor(
+                    out=xs[:],
+                    in0=xb[c][:, j0 * K : (j0 + nj) * K].bitcast(FP8),
+                    in1=sc[:, 0 : nj * K],
+                    op=ALU.mult,
+                )
+            st[("xs", i)] = xs
+
+        def stage_t(i):
+            transposes(i, st[("xs", i)][:], units[i][2])
+
+        def stage_c(i):
+            copy_out(i, units[i][2], lambda h: copy_on_vector(i, h, nu))
+
+        def stage_q(i):
+            nj = units[i][2]
+            xc = work.tile([P, nj * P], U32, name="xc", tag="xc", align_bytes=64)
+            xsc = work.tile([P, nj * P], U8, name="xsc", tag="xsc", align_bytes=64)
+            quantize(i, xc[:], xsc[:])
+            st[("xc", i)] = (xc, xsc)
+
+        wblock = [0, 2, 1, 3]
+
+        def stage_m(i):
+            nj = units[i][2]
+            xc, xsc = st[("xc", i)]
+            width = nj * P
+            if is_half(i, nj):
+                width = 2 * P
+            banks = []
+            for q in range(4):
+                col = q * width
+                if col % W2 == 0:
+                    ps = pm.tile([P, W2], F32, name="ps", tag="ps")
+                    banks.append(ps)
+                wb = wblock[q]
+                nc.tensor.matmul_mx(
+                    out=banks[-1][:, col % W2 : col % W2 + width],
+                    lhsT=wc[:, wb * P : (wb + 1) * P].bitcast(FP8X4),
+                    lhsT_scale=wsc[:, wb * P : (wb + 1) * P],
+                    rhs=xc[:, 0:width].bitcast(FP8X4),
+                    rhs_scale=xsc[:, 0:width],
+                    start=True,
+                    stop=True,
+                )
+            if is_half(i, nj):
+                for j in range(2, 4):
+                    ps = pm.tile([P, W2], F32, name="ps", tag="ps")
+                    banks.append(ps)
+                    nc.tensor.matmul_mx(
+                        out=ps[:],
+                        lhsT=xc[:, j * P : (j + 1) * P].bitcast(FP8X4),
+                        lhsT_scale=xsc[:, j * P : (j + 1) * P],
+                        rhs=wc[:].bitcast(FP8X4),
+                        rhs_scale=wsc[:],
+                        start=True,
+                        stop=True,
+                    )
+            st[("ps", i)] = banks
+
+        def stage_s(i):
+            nj = units[i][2]
+            sq = work.tile([P, nj * W2], F32, name="sq", tag="sq")
+            for j, ps in enumerate(st[("ps", i)]):
+                nc.scalar.activation(out=sq[:, j * W2 : (j + 1) * W2], in_=ps[:], func=ACT.Square)
+            st[("sq", i)] = sq
+
+        def stage_b(i):
+            nj = units[i][2]
+            sq = st[("sq", i)]
+            if is_half(i, nj):
+                nj = 2
+            width = nj * P
+            banks = []
+            for j in range(nj):
+                if j % 2 == 0:
+                    ob = po.tile([P, W2], F32, name="ob", tag="ob")
+                    banks.append(ob)
+                for cb in range(2):
+                    dst = banks[-1][:, (j % 2) * N + cb * P : (j % 2) * N + (cb + 1) * P]
+                    for part in range(2):
+                        col = (2 * cb + part) * width + j * P
+                        nc.tensor.matmul(
+                            out=dst,
+                            lhsT=sq[:, col : col + P],
+                            rhs=ident[:],
+                            is_transpose=True,
+                            start=(part == 0),
+                            stop=(part == 1),
+                        )
+            st[("ob", i)] = banks
+
+        def stage_a(i):
+            nj = units[i][2]
+            if is_half(i, nj):
+                sm = work.tile([P, 2 * N], F32, name="sm", tag="sm")
+                sqv = st[("sq", i)][:, 2 * W2 : 4 * W2].rearrange("p (j c n) -> p j c n", j=2, c=2)
+                nc.vector.tensor_tensor(
+                    out=sm[:].rearrange("p (j n) -> p j n", j=2),
+                    in0=sqv[:, :, 0, :],
+                    in1=sqv[:, :, 1, :],
+                    op=ALU.add,
+                )
+                st[("sm", i)] = sm
+
+        def stage_l(i):
+            c, j0, nj = units[i]
+            ot = outp.tile([P, nj * N], F32, name="ot", tag="ot")
+            for h, ob in enumerate(st[("ob", i)]):
+                width = min(2, nj - 2 * h) * N
+                nc.scalar.activation(out=ot[:, h * W2 : h * W2 + width], in_=ob[:, 0:width], func=ACT.Ln)
+            if is_half(i, nj):
+                nc.scalar.activation(out=ot[:, W2 : 2 * W2], in_=st[("sm", i)][:], func=ACT.Ln)
+            nc.sync.dma_start(out=ov[c][:, j0 : j0 + nj, :], in_=ot[:].rearrange("p (j n) -> p j n", j=nj))
+
+        def ok(i):
+            return 0 <= i < nu
+
+        transposes("w", wp[:], 4)
+        copy_out("w", 4, lambda h: False)
+
+        for n in range(nu + 4):
+            if ok(n - 2):
+                stage_c(n - 2)
+            if ok(n - 3):
+                stage_m(n - 3)
+            if ok(n - 4):
+                stage_b(n - 4)
+            if ok(n - 1):
+                stage_t(n - 1)
+            if ok(n - 4):
+                stage_a(n - 4)
+            if ok(n):
+                stage_p(n)
+            if n == 2:
+                quantize("w", wc[:], wsc[:])
+            if ok(n - 2):
+                stage_q(n - 2)
+            if ok(n - 3):
+                stage_s(n - 3)
+            if ok(n - 4):
+                stage_l(n - 4)

@@ -67,7 +67,7 @@ def tile_dft_kernel(tc, x_bytes, x_scale, dft_real, dft_imag, out):
     with ExitStack() as ctx:
         const = ctx.enter_context(tc.tile_pool(name="const", bufs=1))
         bpool = ctx.enter_context(tc.tile_pool(name="bpool", bufs=NCH))
-        work = ctx.enter_context(tc.tile_pool(name="work", bufs=3))
+        work = ctx.enter_context(tc.tile_pool(name="work", bufs=4))
         outp = ctx.enter_context(tc.tile_pool(name="outp", bufs=8))
         px = ctx.enter_context(tc.psum_pool(name="px", bufs=2))
         pm = ctx.enter_context(tc.psum_pool(name="pm", bufs=4))
@@ -288,24 +288,24 @@ def tile_dft_kernel(tc, x_bytes, x_scale, dft_real, dft_imag, out):
         transposes("w", wp[:], 4)
         copy_out("w", 4, lambda h: False)
 
-        for n in range(nu + 4):
+        for n in range(nu + 5):
             if ok(n - 2):
                 stage_c(n - 2)
-            if ok(n - 3):
-                stage_m(n - 3)
             if ok(n - 4):
-                stage_b(n - 4)
+                stage_m(n - 4)
+            if ok(n - 5):
+                stage_b(n - 5)
             if ok(n - 1):
                 stage_t(n - 1)
-            if ok(n - 4):
-                stage_a(n - 4)
-            if ok(n):
-                stage_p(n)
             if n == 2:
                 quantize("w", wc[:], wsc[:])
-            if ok(n - 2):
-                stage_q(n - 2)
             if ok(n - 3):
-                stage_s(n - 3)
+                stage_q(n - 3)
+            if ok(n - 5):
+                stage_a(n - 5)
+            if ok(n):
+                stage_p(n)
             if ok(n - 4):
-                stage_l(n - 4)
+                stage_s(n - 4)
+            if ok(n - 5):
+                stage_l(n - 5)

@@ -19,7 +19,7 @@ P = 128
 SUB = 4
 NCH = B // (P * SUB)
 W2 = 2 * N
-PERM = False
+CW = 512
 
 
 HEAD = [[2, 2], [2, 2]]
@@ -38,23 +38,7 @@ def unit_list():
 
 
 def is_half(i, nj):
-    return nj == 4 and i % 3 == 1
-
-
-def copy_on_vector(i, h, nu):
-    if i >= nu - 4:
-        return True
-    if i < 6:
-        return False
-    return i % 3 != 0
-
-
-def permuted(ap):
-    return ap.rearrange("p (w g i) -> p g w i", w=2, i=16)
-
-
-def plain(ap):
-    return ap.rearrange("p (g w i) -> p g w i", w=2, i=16)
+    return nj == 4
 
 
 def tile_dft_kernel(tc, x_bytes, x_scale, dft_real, dft_imag, out):
@@ -74,9 +58,7 @@ def tile_dft_kernel(tc, x_bytes, x_scale, dft_real, dft_imag, out):
         po = ctx.enter_context(tc.psum_pool(name="po", bufs=2))
         ctx.enter_context(tc.manual_schedule())
 
-        sc = const.tile([P, SUB * K], F32, name="sc")
-        nc.sync.dma_start(out=sc[:, 0:K], in_=x_scale.rearrange("o k -> (o k)").partition_broadcast(P))
-
+        s4 = const.tile([P, 4], F32, name="s4")
         wr = const.tile([P, 4 * K], BF16, name="wr")
         xb = []
         for c in range(NCH):
@@ -84,6 +66,7 @@ def tile_dft_kernel(tc, x_bytes, x_scale, dft_real, dft_imag, out):
             nc.sync.dma_start(out=xbytes[:].rearrange("p (j k) -> p j k", j=SUB), in_=xv[c])
             xb.append(xbytes)
             if c == 0:
+                nc.sync.dma_start(out=s4[:], in_=x_scale.rearrange("o (p t) -> p (o t)", t=4))
                 nc.sync.dma_start(
                     out=wr[:, 0 : 2 * K].rearrange("p (b k) -> p b k", b=2),
                     in_=dft_real.rearrange("(b p) k -> p b k", p=P),
@@ -99,17 +82,6 @@ def tile_dft_kernel(tc, x_bytes, x_scale, dft_real, dft_imag, out):
         nc.vector.memset(one[:], 1.0)
         warm = const.tile([P, 1], F32, name="warm")
         nc.scalar.activation(out=warm[:], in_=one[:], func=ACT.Ln)
-        if PERM:
-            wp = const.tile([P, 4 * K], BF16, name="wp")
-            for half in range(2):
-                nc.scalar.copy(
-                    out=permuted(wp[:])[:, half * 32 : (half + 1) * 32, :, :],
-                    in_=plain(wr[:])[:, half * 32 : (half + 1) * 32, :, :],
-                )
-        else:
-            wp = wr
-        nc.scalar.copy(out=sc[:, K : 2 * K], in_=sc[:, 0:K])
-        nc.scalar.copy(out=sc[:, 2 * K : 4 * K], in_=sc[:, 0 : 2 * K])
 
         wc = const.tile([P, W2], U32, name="wc", align_bytes=64)
         wsc = const.tile([P, W2], U8, name="wsc", align_bytes=64)
@@ -120,29 +92,32 @@ def tile_dft_kernel(tc, x_bytes, x_scale, dft_real, dft_imag, out):
             words = src.bitcast(F32)
             banks = []
             for h in range((nj + 1) // 2):
-                xt = px.tile([P, 2, 2, P], F32, name="xt", tag="xt")
+                xt = px.tile([P, 2, 2 * P], F32, name="xt", tag="xt")
                 for jj in range(min(2, nj - 2 * h)):
                     j = 2 * h + jj
                     for w in range(2):
-                        if PERM:
-                            cols = words[:, (w * nj + j) * P : (w * nj + j + 1) * P]
-                        else:
-                            cols = words[:, 256 * j + w : 256 * (j + 1) : 2]
-                        nc.tensor.transpose(xt[:, jj, w, :], cols, ident[:])
+                        cols = words[:, 256 * j + w : 256 * (j + 1) : 2]
+                        nc.tensor.transpose(xt[:, w, jj * P : (jj + 1) * P], cols, ident[:])
                 banks.append(xt)
             st[("xt", key)] = banks
 
-        def copy_out(key, nj, on_vector):
+        def copy_out(key, nj, scaled):
             gx = work.tile([P, nj * 4 * P], BF16, name="gx", tag="gx", align_bytes=64)
             gw = gx[:].bitcast(F32)
             for h, xt in enumerate(st[("xt", key)]):
-                njj = min(2, nj - 2 * h)
-                dst = gw[:, 512 * h : 512 * h + 256 * njj].rearrange("p (j r w) -> p j r w", j=njj, w=2)
-                src = xt[:, 0:njj, :, :].rearrange("p j w r -> p j r w")
-                if on_vector(h):
-                    nc.vector.tensor_copy(out=dst, in_=src)
+                rows = min(2, nj - 2 * h) * P
+                if scaled:
+                    nc.vector.tensor_tensor(
+                        out=gx[:, 1024 * h : 1024 * h + 4 * rows].rearrange("p (r w e) -> p r w e", w=2, e=2),
+                        in0=xt[:].bitcast(BF16)[:, :, 0 : 2 * rows].rearrange("p w (r e) -> p r w e", e=2),
+                        in1=s4[:].unsqueeze(1).to_broadcast([P, rows, 4]).rearrange("p r (w e) -> p r w e", w=2),
+                        op=ALU.mult,
+                    )
                 else:
-                    nc.scalar.copy(out=dst, in_=src)
+                    nc.scalar.copy(
+                        out=gw[:, 512 * h : 512 * h + 2 * rows].rearrange("p (r w) -> p r w", w=2),
+                        in_=xt[:, :, 0:rows].rearrange("p w r -> p r w"),
+                    )
             st[("gx", key)] = gx
 
         def quantize(key, codes, scales):
@@ -151,35 +126,19 @@ def tile_dft_kernel(tc, x_bytes, x_scale, dft_real, dft_imag, out):
         def stage_p(i):
             c, j0, nj = units[i]
             xs = work.tile([P, nj * K], BF16, name="xs", tag="xs")
-            if PERM:
-                nc.vector.tensor_tensor(
-                    out=permuted(xs[:]),
-                    in0=plain(xb[c][:, j0 * K : (j0 + nj) * K].bitcast(FP8)),
-                    in1=plain(sc[:, 0 : nj * K]),
-                    op=ALU.mult,
-                )
-            elif c == 0:
-                for j in range(nj):
-                    nc.vector.tensor_tensor(
-                        out=xs[:, j * K : (j + 1) * K],
-                        in0=xb[c][:, (j0 + j) * K : (j0 + j + 1) * K].bitcast(FP8),
-                        in1=sc[:, 0:K],
-                        op=ALU.mult,
-                    )
-            else:
-                nc.vector.tensor_tensor(
-                    out=xs[:],
-                    in0=xb[c][:, j0 * K : (j0 + nj) * K].bitcast(FP8),
-                    in1=sc[:, 0 : nj * K],
-                    op=ALU.mult,
-                )
+            for col in range(0, nj * K, CW):
+                piece = xb[c][:, j0 * K + col : j0 * K + col + CW].bitcast(FP8)
+                if i == 0:
+                    nc.vector.tensor_copy(out=xs[:, col : col + CW], in_=piece)
+                else:
+                    nc.gpsimd.tensor_copy(out=xs[:, col : col + CW], in_=piece)
             st[("xs", i)] = xs
 
         def stage_t(i):
             transposes(i, st[("xs", i)][:], units[i][2])
 
         def stage_c(i):
-            copy_out(i, units[i][2], lambda h: copy_on_vector(i, h, nu))
+            copy_out(i, units[i][2], True)
 
         def stage_q(i):
             nj = units[i][2]
@@ -285,8 +244,8 @@ def tile_dft_kernel(tc, x_bytes, x_scale, dft_real, dft_imag, out):
         def ok(i):
             return 0 <= i < nu
 
-        transposes("w", wp[:], 4)
-        copy_out("w", 4, lambda h: False)
+        transposes("w", wr[:], 4)
+        copy_out("w", 4, False)
 
         for n in range(nu + 5):
             if ok(n - 2):

@@ -38,7 +38,7 @@ def unit_list():
 
 
 def is_half(i, nj):
-    return nj == 4
+    return nj == 4 and i % 2 == 0
 
 
 def tile_dft_kernel(tc, x_bytes, x_scale, dft_real, dft_imag, out):
@@ -52,10 +52,11 @@ def tile_dft_kernel(tc, x_bytes, x_scale, dft_real, dft_imag, out):
         const = ctx.enter_context(tc.tile_pool(name="const", bufs=1))
         bpool = ctx.enter_context(tc.tile_pool(name="bpool", bufs=NCH))
         work = ctx.enter_context(tc.tile_pool(name="work", bufs=4))
+        ring = ctx.enter_context(tc.tile_pool(name="ring", bufs=1))
         outp = ctx.enter_context(tc.tile_pool(name="outp", bufs=8))
-        px = ctx.enter_context(tc.psum_pool(name="px", bufs=2))
+        px = ctx.enter_context(tc.psum_pool(name="px", bufs=3))
         pm = ctx.enter_context(tc.psum_pool(name="pm", bufs=4))
-        po = ctx.enter_context(tc.psum_pool(name="po", bufs=2))
+        po = ctx.enter_context(tc.psum_pool(name="po", bufs=1))
         ctx.enter_context(tc.manual_schedule())
 
         s4 = const.tile([P, 4], F32, name="s4")
@@ -102,7 +103,8 @@ def tile_dft_kernel(tc, x_bytes, x_scale, dft_real, dft_imag, out):
             st[("xt", key)] = banks
 
         def copy_out(key, nj, scaled):
-            gx = work.tile([P, nj * 4 * P], BF16, name="gx", tag="gx", align_bytes=64)
+            slot = 4 if key == "w" else key % 4
+            gx = ring.tile([P, SUB * K], BF16, name="gx", tag="ring%d" % slot, align_bytes=64)
             gw = gx[:].bitcast(F32)
             for h, xt in enumerate(st[("xt", key)]):
                 rows = min(2, nj - 2 * h) * P
@@ -120,22 +122,22 @@ def tile_dft_kernel(tc, x_bytes, x_scale, dft_real, dft_imag, out):
                     )
             st[("gx", key)] = gx
 
-        def quantize(key, codes, scales):
-            nc.vector.quantize_mx(out=codes.bitcast(FP8X4), scales=scales, in_=st[("gx", key)][:])
+        def quantize(key, nj, codes, scales):
+            nc.vector.quantize_mx(out=codes.bitcast(FP8X4), scales=scales, in_=st[("gx", key)][:, 0 : 4 * nj * P])
 
         def stage_p(i):
             c, j0, nj = units[i]
-            xs = work.tile([P, nj * K], BF16, name="xs", tag="xs")
+            xs = ring.tile([P, SUB * K], BF16, name="xs", tag="ring%d" % ((i + 1) % 4), align_bytes=64)
             for col in range(0, nj * K, CW):
                 piece = xb[c][:, j0 * K + col : j0 * K + col + CW].bitcast(FP8)
-                if i == 0:
+                if i == 0 or col < 512:
                     nc.vector.tensor_copy(out=xs[:, col : col + CW], in_=piece)
                 else:
                     nc.gpsimd.tensor_copy(out=xs[:, col : col + CW], in_=piece)
             st[("xs", i)] = xs
 
         def stage_t(i):
-            transposes(i, st[("xs", i)][:], units[i][2])
+            transposes(i, st[("xs", i)][:, 0 : units[i][2] * K], units[i][2])
 
         def stage_c(i):
             copy_out(i, units[i][2], True)
@@ -144,7 +146,7 @@ def tile_dft_kernel(tc, x_bytes, x_scale, dft_real, dft_imag, out):
             nj = units[i][2]
             xc = work.tile([P, nj * P], U32, name="xc", tag="xc", align_bytes=64)
             xsc = work.tile([P, nj * P], U8, name="xsc", tag="xsc", align_bytes=64)
-            quantize(i, xc[:], xsc[:])
+            quantize(i, nj, xc[:], xsc[:])
             st[("xc", i)] = (xc, xsc)
 
         wblock = [0, 2, 1, 3]
@@ -248,6 +250,12 @@ def tile_dft_kernel(tc, x_bytes, x_scale, dft_real, dft_imag, out):
         copy_out("w", 4, False)
 
         for n in range(nu + 5):
+            if ok(n - 5):
+                stage_a(n - 5)
+            if ok(n - 3):
+                stage_q(n - 3)
+            if n == 2:
+                quantize("w", 4, wc[:], wsc[:])
             if ok(n - 2):
                 stage_c(n - 2)
             if ok(n - 4):
@@ -256,12 +264,6 @@ def tile_dft_kernel(tc, x_bytes, x_scale, dft_real, dft_imag, out):
                 stage_b(n - 5)
             if ok(n - 1):
                 stage_t(n - 1)
-            if n == 2:
-                quantize("w", wc[:], wsc[:])
-            if ok(n - 3):
-                stage_q(n - 3)
-            if ok(n - 5):
-                stage_a(n - 5)
             if ok(n):
                 stage_p(n)
             if ok(n - 4):

@@ -20,6 +20,10 @@ SUB = 4
 NCH = B // (P * SUB)
 W2 = 2 * N
 CW = 512
+PRO, WB, TA, VH, VX, VS = 0, False, 2, 8, 512, 3
+RS = lambda i: 1
+RS2 = lambda i: 0
+ND, WP, T0F, SQV, LATE, QW = 6, True, 0, 3, 99, 3
 
 
 HEAD = [[2, 2], [2, 2]]
@@ -37,8 +41,15 @@ def unit_list():
     return units
 
 
-def is_half(i, nj):
-    return nj == 4 and i % 2 == 0
+def resident(i, nj):
+    return RS(i) if nj == 4 else RS2(i)
+
+
+def spot(q, j, ws):
+    if ws == 3 and j == 2:
+        return 8 * P + q * P
+    width = min(ws, 4) if ws != 3 else 2
+    return (q * width + j) * P
 
 
 def tile_dft_kernel(tc, x_bytes, x_scale, dft_real, dft_imag, out):
@@ -54,12 +65,15 @@ def tile_dft_kernel(tc, x_bytes, x_scale, dft_real, dft_imag, out):
         work = ctx.enter_context(tc.tile_pool(name="work", bufs=4))
         ring = ctx.enter_context(tc.tile_pool(name="ring", bufs=1))
         outp = ctx.enter_context(tc.tile_pool(name="outp", bufs=8))
-        px = ctx.enter_context(tc.psum_pool(name="px", bufs=3))
+        px = ctx.enter_context(tc.psum_pool(name="px", bufs=2))
         pm = ctx.enter_context(tc.psum_pool(name="pm", bufs=4))
-        po = ctx.enter_context(tc.psum_pool(name="po", bufs=1))
+        po = ctx.enter_context(tc.psum_pool(name="po", bufs=2))
         ctx.enter_context(tc.manual_schedule())
 
         s4 = const.tile([P, 4], F32, name="s4")
+        if ND > 0:
+            sc = const.tile([P, K], F32, name="sc")
+            nc.sync.dma_start(out=sc[:], in_=x_scale.rearrange("o k -> (o k)").partition_broadcast(P))
         wr = const.tile([P, 4 * K], BF16, name="wr")
         xb = []
         for c in range(NCH):
@@ -93,7 +107,10 @@ def tile_dft_kernel(tc, x_bytes, x_scale, dft_real, dft_imag, out):
             words = src.bitcast(F32)
             banks = []
             for h in range((nj + 1) // 2):
-                xt = px.tile([P, 2, 2 * P], F32, name="xt", tag="xt")
+                if key == "w" and WP:
+                    xt = po.tile([P, 2, 2 * P], F32, name="xt", tag="ob")
+                else:
+                    xt = px.tile([P, 2, 2 * P], F32, name="xt", tag="xt")
                 for jj in range(min(2, nj - 2 * h)):
                     j = 2 * h + jj
                     for w in range(2):
@@ -128,9 +145,17 @@ def tile_dft_kernel(tc, x_bytes, x_scale, dft_real, dft_imag, out):
         def stage_p(i):
             c, j0, nj = units[i]
             xs = ring.tile([P, SUB * K], BF16, name="xs", tag="ring%d" % ((i + 1) % 4), align_bytes=64)
-            for col in range(0, nj * K, CW):
+            if i < ND:
+                for col in range(0, nj * K, K):
+                    nc.vector.tensor_tensor(
+                        out=xs[:, col : col + K],
+                        in0=xb[c][:, j0 * K + col : j0 * K + col + K].bitcast(FP8),
+                        in1=sc[:],
+                        op=ALU.mult,
+                    )
+            for col in range(0, nj * K if i >= ND else 0, CW):
                 piece = xb[c][:, j0 * K + col : j0 * K + col + CW].bitcast(FP8)
-                if i == 0 or col < 512:
+                if i < VH or (col < VX and i >= VS):
                     nc.vector.tensor_copy(out=xs[:, col : col + CW], in_=piece)
                 else:
                     nc.gpsimd.tensor_copy(out=xs[:, col : col + CW], in_=piece)
@@ -140,7 +165,7 @@ def tile_dft_kernel(tc, x_bytes, x_scale, dft_real, dft_imag, out):
             transposes(i, st[("xs", i)][:, 0 : units[i][2] * K], units[i][2])
 
         def stage_c(i):
-            copy_out(i, units[i][2], True)
+            copy_out(i, units[i][2], i >= ND)
 
         def stage_q(i):
             nj = units[i][2]
@@ -154,62 +179,66 @@ def tile_dft_kernel(tc, x_bytes, x_scale, dft_real, dft_imag, out):
         def stage_m(i):
             nj = units[i][2]
             xc, xsc = st[("xc", i)]
-            width = nj * P
-            if is_half(i, nj):
-                width = 2 * P
+            rs = resident(i, nj)
+            ws = nj - rs
+            runs = {4: [(0, 4)], 3: [(0, 2), (2, 1)], 2: [(0, 2)], 1: [(0, 1)], 0: []}[ws]
             banks = []
-            for q in range(4):
-                col = q * width
-                if col % W2 == 0:
-                    ps = pm.tile([P, W2], F32, name="ps", tag="ps")
-                    banks.append(ps)
-                wb = wblock[q]
-                nc.tensor.matmul_mx(
-                    out=banks[-1][:, col % W2 : col % W2 + width],
-                    lhsT=wc[:, wb * P : (wb + 1) * P].bitcast(FP8X4),
-                    lhsT_scale=wsc[:, wb * P : (wb + 1) * P],
-                    rhs=xc[:, 0:width].bitcast(FP8X4),
-                    rhs_scale=xsc[:, 0:width],
-                    start=True,
-                    stop=True,
-                )
-            if is_half(i, nj):
-                for j in range(2, 4):
-                    ps = pm.tile([P, W2], F32, name="ps", tag="ps")
-                    banks.append(ps)
+            for j, nw in runs:
+                for q in range(4):
+                    col = spot(q, j, ws)
+                    if col % W2 == 0:
+                        ps = pm.tile([P, W2], F32, name="ps", tag="ps")
+                        banks.append(ps)
+                    wb = wblock[q]
                     nc.tensor.matmul_mx(
-                        out=ps[:],
-                        lhsT=xc[:, j * P : (j + 1) * P].bitcast(FP8X4),
-                        lhsT_scale=xsc[:, j * P : (j + 1) * P],
-                        rhs=wc[:].bitcast(FP8X4),
-                        rhs_scale=wsc[:],
+                        out=banks[-1][:, col % W2 : col % W2 + nw * P],
+                        lhsT=wc[:, wb * P : (wb + 1) * P].bitcast(FP8X4),
+                        lhsT_scale=wsc[:, wb * P : (wb + 1) * P],
+                        rhs=xc[:, j * P : (j + nw) * P].bitcast(FP8X4),
+                        rhs_scale=xsc[:, j * P : (j + nw) * P],
                         start=True,
                         stop=True,
                     )
+            for j in range(ws, nj):
+                ps = pm.tile([P, W2], F32, name="ps", tag="ps")
+                banks.append(ps)
+                nc.tensor.matmul_mx(
+                    out=ps[:],
+                    lhsT=xc[:, j * P : (j + 1) * P].bitcast(FP8X4),
+                    lhsT_scale=xsc[:, j * P : (j + 1) * P],
+                    rhs=wc[:].bitcast(FP8X4),
+                    rhs_scale=wsc[:],
+                    start=True,
+                    stop=True,
+                )
             st[("ps", i)] = banks
 
         def stage_s(i):
             nj = units[i][2]
             sq = work.tile([P, nj * W2], F32, name="sq", tag="sq")
             for j, ps in enumerate(st[("ps", i)]):
-                nc.scalar.activation(out=sq[:, j * W2 : (j + 1) * W2], in_=ps[:], func=ACT.Square)
+                dst = sq[:, j * W2 : (j + 1) * W2]
+                if i >= nu - SQV and j == len(st[("ps", i)]) - 1:
+                    cp = work.tile([P, W2], F32, name="cp", tag="cp")
+                    nc.vector.tensor_copy(out=cp[:], in_=ps[:])
+                    nc.vector.tensor_tensor(out=dst, in0=ps[:], in1=cp[:], op=ALU.mult)
+                else:
+                    nc.scalar.activation(out=dst, in_=ps[:], func=ACT.Square)
             st[("sq", i)] = sq
 
         def stage_b(i):
             nj = units[i][2]
             sq = st[("sq", i)]
-            if is_half(i, nj):
-                nj = 2
-            width = nj * P
+            ws = nj - resident(i, nj)
             banks = []
-            for j in range(nj):
+            for j in range(ws):
                 if j % 2 == 0:
                     ob = po.tile([P, W2], F32, name="ob", tag="ob")
                     banks.append(ob)
                 for cb in range(2):
                     dst = banks[-1][:, (j % 2) * N + cb * P : (j % 2) * N + (cb + 1) * P]
                     for part in range(2):
-                        col = (2 * cb + part) * width + j * P
+                        col = spot(2 * cb + part, j, ws)
                         nc.tensor.matmul(
                             out=dst,
                             lhsT=sq[:, col : col + P],
@@ -222,11 +251,12 @@ def tile_dft_kernel(tc, x_bytes, x_scale, dft_real, dft_imag, out):
 
         def stage_a(i):
             nj = units[i][2]
-            if is_half(i, nj):
-                sm = work.tile([P, 2 * N], F32, name="sm", tag="sm")
-                sqv = st[("sq", i)][:, 2 * W2 : 4 * W2].rearrange("p (j c n) -> p j c n", j=2, c=2)
+            rs = resident(i, nj)
+            if rs > 0:
+                sm = work.tile([P, rs * N], F32, name="sm", tag="sm")
+                sqv = st[("sq", i)][:, (nj - rs) * W2 : nj * W2].rearrange("p (j c n) -> p j c n", j=rs, c=2)
                 nc.vector.tensor_tensor(
-                    out=sm[:].rearrange("p (j n) -> p j n", j=2),
+                    out=sm[:].rearrange("p (j n) -> p j n", j=rs),
                     in0=sqv[:, :, 0, :],
                     in1=sqv[:, :, 1, :],
                     op=ALU.add,
@@ -236,35 +266,45 @@ def tile_dft_kernel(tc, x_bytes, x_scale, dft_real, dft_imag, out):
         def stage_l(i):
             c, j0, nj = units[i]
             ot = outp.tile([P, nj * N], F32, name="ot", tag="ot")
+            rs = resident(i, nj)
+            ws = nj - rs
             for h, ob in enumerate(st[("ob", i)]):
-                width = min(2, nj - 2 * h) * N
+                width = min(2, ws - 2 * h) * N
                 nc.scalar.activation(out=ot[:, h * W2 : h * W2 + width], in_=ob[:, 0:width], func=ACT.Ln)
-            if is_half(i, nj):
-                nc.scalar.activation(out=ot[:, W2 : 2 * W2], in_=st[("sm", i)][:], func=ACT.Ln)
+            if rs > 0:
+                nc.scalar.activation(out=ot[:, ws * N : nj * N], in_=st[("sm", i)][:], func=ACT.Ln)
             nc.sync.dma_start(out=ov[c][:, j0 : j0 + nj, :], in_=ot[:].rearrange("p (j n) -> p j n", j=nj))
 
         def ok(i):
             return 0 <= i < nu
 
+        for i in range(PRO):
+            stage_p(i)
+        for i in range(T0F):
+            stage_t(i)
         transposes("w", wr[:], 4)
         copy_out("w", 4, False)
 
         for n in range(nu + 5):
-            if ok(n - 5):
+            if ok(n - 5) and n < nu + TA:
                 stage_a(n - 5)
             if ok(n - 3):
                 stage_q(n - 3)
-            if n == 2:
+            if n == QW and WB:
                 quantize("w", 4, wc[:], wsc[:])
             if ok(n - 2):
                 stage_c(n - 2)
+            if n == QW and not WB:
+                quantize("w", 4, wc[:], wsc[:])
+            if ok(n - 5) and n >= nu + TA:
+                stage_a(n - 5)
             if ok(n - 4):
                 stage_m(n - 4)
             if ok(n - 5):
                 stage_b(n - 5)
-            if ok(n - 1):
+            if ok(n - 1) and n - 1 >= T0F:
                 stage_t(n - 1)
-            if ok(n):
+            if ok(n) and n >= PRO:
                 stage_p(n)
             if ok(n - 4):
                 stage_s(n - 4)

@@ -19,11 +19,14 @@ P = 128
 SUB = 4
 NCH = B // (P * SUB)
 W2 = 2 * N
-CW = 512
+CW = 2048
+NV = 1
+ORD = "cqap"
+GL = 0
 PRO, WB, TA, VH, VX, VS = 0, False, 2, 8, 512, 3
 RS = lambda i: 1
 RS2 = lambda i: 0
-ND, WP, T0F, SQV, LATE, QW = 6, True, 0, 3, 99, 3
+ND, WP, T0F, SQV, LATE, QW = 6, True, 0, 4, 99, 3
 
 
 HEAD = [[2, 2], [2, 2]]
@@ -104,7 +107,6 @@ def tile_dft_kernel(tc, x_bytes, x_scale, dft_real, dft_imag, out):
         st = {}
 
         def transposes(key, src, nj):
-            words = src.bitcast(F32)
             banks = []
             for h in range((nj + 1) // 2):
                 if key == "w" and WP:
@@ -114,7 +116,7 @@ def tile_dft_kernel(tc, x_bytes, x_scale, dft_real, dft_imag, out):
                 for jj in range(min(2, nj - 2 * h)):
                     j = 2 * h + jj
                     for w in range(2):
-                        cols = words[:, 256 * j + w : 256 * (j + 1) : 2]
+                        cols = src[j].bitcast(F32)[:, w : 256 : 2]
                         nc.tensor.transpose(xt[:, w, jj * P : (jj + 1) * P], cols, ident[:])
                 banks.append(xt)
             st[("xt", key)] = banks
@@ -144,25 +146,34 @@ def tile_dft_kernel(tc, x_bytes, x_scale, dft_real, dft_imag, out):
 
         def stage_p(i):
             c, j0, nj = units[i]
-            xs = ring.tile([P, SUB * K], BF16, name="xs", tag="ring%d" % ((i + 1) % 4), align_bytes=64)
-            if i < ND:
-                for col in range(0, nj * K, K):
-                    nc.vector.tensor_tensor(
-                        out=xs[:, col : col + K],
-                        in0=xb[c][:, j0 * K + col : j0 * K + col + K].bitcast(FP8),
-                        in1=sc[:],
-                        op=ALU.mult,
-                    )
-            for col in range(0, nj * K if i >= ND else 0, CW):
-                piece = xb[c][:, j0 * K + col : j0 * K + col + CW].bitcast(FP8)
-                if i < VH or (col < VX and i >= VS):
-                    nc.vector.tensor_copy(out=xs[:, col : col + CW], in_=piece)
-                else:
-                    nc.gpsimd.tensor_copy(out=xs[:, col : col + CW], in_=piece)
-            st[("xs", i)] = xs
+            if i < ND or i < VH:
+                xs = work.tile([P, SUB * K], BF16, name="xsd", tag="xsd", bufs=3)
+                for j in range(nj):
+                    piece = xb[c][:, (j0 + j) * K : (j0 + j + 1) * K].bitcast(FP8)
+                    if i < ND:
+                        nc.vector.tensor_tensor(out=xs[:, j * K : (j + 1) * K], in0=piece, in1=sc[:], op=ALU.mult)
+                    elif j == 0:
+                        nc.vector.tensor_copy(out=xs[:, 0 : nj * K], in_=xb[c][:, j0 * K : (j0 + nj) * K].bitcast(FP8))
+                st[("xs", i)] = [xs[:, j * K : (j + 1) * K] for j in range(nj)]
+            else:
+                xs = work.tile([P, NV * K], BF16, name="xsv", tag="xsv")
+                nv = NV if nj == 4 else NV // 2
+                if nv > 0:
+                    nc.vector.tensor_copy(out=xs[:, 0 : nv * K], in_=xb[c][:, j0 * K : (j0 + nv) * K].bitcast(FP8))
+                st[("xs", i)] = [xs[:, j * K : (j + 1) * K] for j in range(nv)]
+
+        def stage_g(i):
+            c, j0, nj = units[i]
+            nv = NV if nj == 4 else NV // 2
+            if i >= ND and i >= VH:
+                xs = ring.tile([P, SUB * K], BF16, name="xs", tag="ring%d" % ((i + 1) % 4), align_bytes=64)
+                for col in range(nv * K, nj * K, CW):
+                    end = min(col + CW, nj * K)
+                    nc.gpsimd.tensor_copy(out=xs[:, col:end], in_=xb[c][:, j0 * K + col : j0 * K + end].bitcast(FP8))
+                st[("xs", i)] += [xs[:, j * K : (j + 1) * K] for j in range(nv, nj)]
 
         def stage_t(i):
-            transposes(i, st[("xs", i)][:, 0 : units[i][2] * K], units[i][2])
+            transposes(i, st[("xs", i)], units[i][2])
 
         def stage_c(i):
             copy_out(i, units[i][2], i >= ND)
@@ -282,30 +293,34 @@ def tile_dft_kernel(tc, x_bytes, x_scale, dft_real, dft_imag, out):
             stage_p(i)
         for i in range(T0F):
             stage_t(i)
-        transposes("w", wr[:], 4)
+        transposes("w", [wr[:, j * K : (j + 1) * K] for j in range(4)], 4)
         copy_out("w", 4, False)
 
+        def vector_turn(n):
+            for step in ORD:
+                if step == "c" and ok(n):
+                    stage_p(n)
+                if step == "q" and ok(n - 3):
+                    stage_q(n - 3)
+                if step == "q" and n == QW:
+                    quantize("w", 4, wc[:], wsc[:])
+                if step == "g" and ok(n):
+                    stage_g(n)
+                if step == "a" and ok(n - 5):
+                    stage_a(n - 5)
+                if step == "p" and ok(n - 2):
+                    stage_c(n - 2)
+
         for n in range(nu + 5):
-            if ok(n - 5) and n < nu + TA:
-                stage_a(n - 5)
-            if ok(n - 3):
-                stage_q(n - 3)
-            if n == QW and WB:
-                quantize("w", 4, wc[:], wsc[:])
-            if ok(n - 2):
-                stage_c(n - 2)
-            if n == QW and not WB:
-                quantize("w", 4, wc[:], wsc[:])
-            if ok(n - 5) and n >= nu + TA:
-                stage_a(n - 5)
+            vector_turn(n)
             if ok(n - 4):
                 stage_m(n - 4)
             if ok(n - 5):
                 stage_b(n - 5)
             if ok(n - 1) and n - 1 >= T0F:
                 stage_t(n - 1)
-            if ok(n) and n >= PRO:
-                stage_p(n)
+            if ok(n) and "g" not in ORD:
+                stage_g(n)
             if ok(n - 4):
                 stage_s(n - 4)
             if ok(n - 5):

@@ -21,8 +21,9 @@ NCH = B // (P * SUB)
 W2 = 2 * N
 CW = 2048
 NV = 1
+NVF = lambda i: NV
 ORD = "cqap"
-GL = 0
+AD = 1
 PRO, WB, TA, VH, VX, VS = 0, False, 2, 8, 512, 3
 RS = lambda i: 1
 RS2 = lambda i: 0
@@ -157,14 +158,14 @@ def tile_dft_kernel(tc, x_bytes, x_scale, dft_real, dft_imag, out):
                 st[("xs", i)] = [xs[:, j * K : (j + 1) * K] for j in range(nj)]
             else:
                 xs = work.tile([P, NV * K], BF16, name="xsv", tag="xsv")
-                nv = NV if nj == 4 else NV // 2
+                nv = NVF(i) if nj == 4 else 0
                 if nv > 0:
                     nc.vector.tensor_copy(out=xs[:, 0 : nv * K], in_=xb[c][:, j0 * K : (j0 + nv) * K].bitcast(FP8))
                 st[("xs", i)] = [xs[:, j * K : (j + 1) * K] for j in range(nv)]
 
         def stage_g(i):
             c, j0, nj = units[i]
-            nv = NV if nj == 4 else NV // 2
+            nv = NVF(i) if nj == 4 else 0
             if i >= ND and i >= VH:
                 xs = ring.tile([P, SUB * K], BF16, name="xs", tag="ring%d" % ((i + 1) % 4), align_bytes=64)
                 for col in range(nv * K, nj * K, CW):
@@ -226,7 +227,7 @@ def tile_dft_kernel(tc, x_bytes, x_scale, dft_real, dft_imag, out):
 
         def stage_s(i):
             nj = units[i][2]
-            sq = work.tile([P, nj * W2], F32, name="sq", tag="sq")
+            sq = work.tile([P, nj * W2], F32, name="sq", tag="sq", bufs=5)
             for j, ps in enumerate(st[("ps", i)]):
                 dst = sq[:, j * W2 : (j + 1) * W2]
                 if i >= nu - SQV and j == len(st[("ps", i)]) - 1:
@@ -282,6 +283,13 @@ def tile_dft_kernel(tc, x_bytes, x_scale, dft_real, dft_imag, out):
             for h, ob in enumerate(st[("ob", i)]):
                 width = min(2, ws - 2 * h) * N
                 nc.scalar.activation(out=ot[:, h * W2 : h * W2 + width], in_=ob[:, 0:width], func=ACT.Ln)
+            st[("ot", i)] = ot
+
+        def stage_o(i):
+            c, j0, nj = units[i]
+            ot = st[("ot", i)]
+            rs = resident(i, nj)
+            ws = nj - rs
             if rs > 0:
                 nc.scalar.activation(out=ot[:, ws * N : nj * N], in_=st[("sm", i)][:], func=ACT.Ln)
             nc.sync.dma_start(out=ov[c][:, j0 : j0 + nj, :], in_=ot[:].rearrange("p (j n) -> p j n", j=nj))
@@ -306,12 +314,12 @@ def tile_dft_kernel(tc, x_bytes, x_scale, dft_real, dft_imag, out):
                     quantize("w", 4, wc[:], wsc[:])
                 if step == "g" and ok(n):
                     stage_g(n)
-                if step == "a" and ok(n - 5):
-                    stage_a(n - 5)
+                if step == "a" and ok(n - 5 - AD):
+                    stage_a(n - 5 - AD)
                 if step == "p" and ok(n - 2):
                     stage_c(n - 2)
 
-        for n in range(nu + 5):
+        for n in range(nu + 5 + AD):
             vector_turn(n)
             if ok(n - 4):
                 stage_m(n - 4)
@@ -325,3 +333,5 @@ def tile_dft_kernel(tc, x_bytes, x_scale, dft_real, dft_imag, out):
                 stage_s(n - 4)
             if ok(n - 5):
                 stage_l(n - 5)
+            if ok(n - 5 - AD):
+                stage_o(n - 5 - AD)

@@ -25,7 +25,7 @@ NVF = lambda i: NV
 ORD = "cqap"
 AD = 1
 PRO, WB, TA, VH, VX, VS = 0, False, 2, 8, 512, 3
-RS = lambda i: 1
+RS = lambda i: 1+i%2
 RS2 = lambda i: 0
 ND, WP, T0F, SQV, LATE, QW = 6, True, 0, 4, 99, 3
 

@@ -21,12 +21,12 @@ NCH = B // (P * SUB)
 W2 = 2 * N
 CW = 2048
 NV = 1
-NVF = lambda i: NV
-ORD = "cqap"
+NVF = lambda i: i%2
+ORD = "caqp"
 AD = 1
 PRO, WB, TA, VH, VX, VS = 0, False, 2, 8, 512, 3
-RS = lambda i: 1+i%2
-RS2 = lambda i: 0
+RS = lambda i: 1+(i%3>0)
+RS2 = lambda i: 1
 ND, WP, T0F, SQV, LATE, QW = 6, True, 0, 4, 99, 3
 
 
@@ -167,7 +167,7 @@ def tile_dft_kernel(tc, x_bytes, x_scale, dft_real, dft_imag, out):
             c, j0, nj = units[i]
             nv = NVF(i) if nj == 4 else 0
             if i >= ND and i >= VH:
-                xs = ring.tile([P, SUB * K], BF16, name="xs", tag="ring%d" % ((i + 1) % 4), align_bytes=64)
+                xs = ring.tile([P, SUB * K], BF16, name="xs", tag="squares%d" % ((i + 2) % 4), align_bytes=64)
                 for col in range(nv * K, nj * K, CW):
                     end = min(col + CW, nj * K)
                     nc.gpsimd.tensor_copy(out=xs[:, col:end], in_=xb[c][:, j0 * K + col : j0 * K + end].bitcast(FP8))
@@ -227,7 +227,7 @@ def tile_dft_kernel(tc, x_bytes, x_scale, dft_real, dft_imag, out):
 
         def stage_s(i):
             nj = units[i][2]
-            sq = work.tile([P, nj * W2], F32, name="sq", tag="sq", bufs=5)
+            sq = ring.tile([P, nj * W2], F32, name="sq", tag="squares%d" % (i % 4), align_bytes=64)
             for j, ps in enumerate(st[("ps", i)]):
                 dst = sq[:, j * W2 : (j + 1) * W2]
                 if i >= nu - SQV and j == len(st[("ps", i)]) - 1:

@@ -20,12 +20,12 @@ SUB = 4
 NCH = B // (P * SUB)
 W2 = 2 * N
 CW = 2048
-NV = 1
-NVF = lambda i: i%2
+NV = 0
+NVF = lambda i: NV
 ORD = "caqp"
 AD = 1
 PRO, WB, TA, VH, VX, VS = 0, False, 2, 8, 512, 3
-RS = lambda i: 1+(i%3>0)
+RS = lambda i: 1+i%2
 RS2 = lambda i: 1
 ND, WP, T0F, SQV, LATE, QW = 6, True, 0, 4, 99, 3
 

@@ -24,6 +24,8 @@ NV = 0
 NVF = lambda i: NV
 ORD = "caqp"
 AD = 1
+SPLIT = True
+HALFLOAD = 2
 PRO, WB, TA, VH, VX, VS = 0, False, 2, 8, 512, 3
 RS = lambda i: 1+i%2
 RS2 = lambda i: 1
@@ -75,17 +77,20 @@ def tile_dft_kernel(tc, x_bytes, x_scale, dft_real, dft_imag, out):
         ctx.enter_context(tc.manual_schedule())
 
         s4 = const.tile([P, 4], F32, name="s4")
-        if ND > 0:
-            sc = const.tile([P, K], F32, name="sc")
-            nc.sync.dma_start(out=sc[:], in_=x_scale.rearrange("o k -> (o k)").partition_broadcast(P))
+        nc.sync.dma_start(out=s4[:], in_=x_scale.rearrange("o (p t) -> p (o t)", t=4))
+        sc = const.tile([P, K], F32, name="sc")
         wr = const.tile([P, 4 * K], BF16, name="wr")
         xb = []
         for c in range(NCH):
             xbytes = bpool.tile([P, SUB * K], U8, name="xbytes", tag="xbytes")
-            nc.sync.dma_start(out=xbytes[:].rearrange("p (j k) -> p j k", j=SUB), in_=xv[c])
+            step = HALFLOAD if c == 0 else SUB
+            for j in range(0, SUB, step):
+                nc.sync.dma_start(
+                    out=xbytes[:, j * K : (j + step) * K].rearrange("p (j k) -> p j k", j=step),
+                    in_=xv[c][:, j : j + step, :],
+                )
             xb.append(xbytes)
             if c == 0:
-                nc.sync.dma_start(out=s4[:], in_=x_scale.rearrange("o (p t) -> p (o t)", t=4))
                 nc.sync.dma_start(
                     out=wr[:, 0 : 2 * K].rearrange("p (b k) -> p b k", b=2),
                     in_=dft_real.rearrange("(b p) k -> p b k", p=P),
@@ -233,6 +238,9 @@ def tile_dft_kernel(tc, x_bytes, x_scale, dft_real, dft_imag, out):
                 if i >= nu - SQV and j == len(st[("ps", i)]) - 1:
                     cp = work.tile([P, W2], F32, name="cp", tag="cp")
                     nc.vector.tensor_copy(out=cp[:], in_=ps[:])
+                    if SPLIT:
+                        if ok(i - 1):
+                            stage_a(i - 1)
                     nc.vector.tensor_tensor(out=dst, in0=ps[:], in1=cp[:], op=ALU.mult)
                 else:
                     nc.scalar.activation(out=dst, in_=ps[:], func=ACT.Square)
@@ -297,6 +305,13 @@ def tile_dft_kernel(tc, x_bytes, x_scale, dft_real, dft_imag, out):
         def ok(i):
             return 0 <= i < nu
 
+        spread = po.tile([P, 4, P], F32, name="spread", tag="ob")
+        for t in range(4):
+            nc.tensor.transpose(spread[:, t, :], s4[:, t : t + 1].to_broadcast([P, P]), ident[:])
+        nc.scalar.copy(
+            out=sc[:].rearrange("p (n t) -> p n t", t=4),
+            in_=spread[:].rearrange("p t n -> p n t"),
+        )
         for i in range(PRO):
             stage_p(i)
         for i in range(T0F):
@@ -314,7 +329,7 @@ def tile_dft_kernel(tc, x_bytes, x_scale, dft_real, dft_imag, out):
                     quantize("w", 4, wc[:], wsc[:])
                 if step == "g" and ok(n):
                     stage_g(n)
-                if step == "a" and ok(n - 5 - AD):
+                if step == "a" and ok(n - 5 - AD) and not (SPLIT and n - 5 - AD >= nu - SQV - 1 and n - 5 - AD < nu - 1):
                     stage_a(n - 5 - AD)
                 if step == "p" and ok(n - 2):
                     stage_c(n - 2)

@@ -25,6 +25,7 @@ NVF = lambda i: NV
 ORD = "caqp"
 AD = 1
 SPLIT = True
+FD = 0
 HALFLOAD = 2
 PRO, WB, TA, VH, VX, VS = 0, False, 2, 8, 512, 3
 RS = lambda i: 1+i%2
@@ -45,6 +46,10 @@ def unit_list():
             units.append((c, j0, nj))
             j0 += nj
     return units
+
+
+def direct(i):
+    return FD <= i < ND
 
 
 def resident(i, nj):
@@ -152,11 +157,11 @@ def tile_dft_kernel(tc, x_bytes, x_scale, dft_real, dft_imag, out):
 
         def stage_p(i):
             c, j0, nj = units[i]
-            if i < ND or i < VH:
+            if i < VH:
                 xs = work.tile([P, SUB * K], BF16, name="xsd", tag="xsd", bufs=3)
                 for j in range(nj):
                     piece = xb[c][:, (j0 + j) * K : (j0 + j + 1) * K].bitcast(FP8)
-                    if i < ND:
+                    if direct(i):
                         nc.vector.tensor_tensor(out=xs[:, j * K : (j + 1) * K], in0=piece, in1=sc[:], op=ALU.mult)
                     elif j == 0:
                         nc.vector.tensor_copy(out=xs[:, 0 : nj * K], in_=xb[c][:, j0 * K : (j0 + nj) * K].bitcast(FP8))
@@ -171,7 +176,7 @@ def tile_dft_kernel(tc, x_bytes, x_scale, dft_real, dft_imag, out):
         def stage_g(i):
             c, j0, nj = units[i]
             nv = NVF(i) if nj == 4 else 0
-            if i >= ND and i >= VH:
+            if i >= VH:
                 xs = ring.tile([P, SUB * K], BF16, name="xs", tag="squares%d" % ((i + 2) % 4), align_bytes=64)
                 for col in range(nv * K, nj * K, CW):
                     end = min(col + CW, nj * K)
@@ -182,7 +187,7 @@ def tile_dft_kernel(tc, x_bytes, x_scale, dft_real, dft_imag, out):
             transposes(i, st[("xs", i)], units[i][2])
 
         def stage_c(i):
-            copy_out(i, units[i][2], i >= ND)
+            copy_out(i, units[i][2], not direct(i))
 
         def stage_q(i):
             nj = units[i][2]
@@ -305,6 +310,8 @@ def tile_dft_kernel(tc, x_bytes, x_scale, dft_real, dft_imag, out):
         def ok(i):
             return 0 <= i < nu
 
+        if T0F:
+            stage_p(0)
         spread = po.tile([P, 4, P], F32, name="spread", tag="ob")
         for t in range(4):
             nc.tensor.transpose(spread[:, t, :], s4[:, t : t + 1].to_broadcast([P, P]), ident[:])
@@ -321,7 +328,7 @@ def tile_dft_kernel(tc, x_bytes, x_scale, dft_real, dft_imag, out):
 
         def vector_turn(n):
             for step in ORD:
-                if step == "c" and ok(n):
+                if step == "c" and ok(n) and n >= T0F:
                     stage_p(n)
                 if step == "q" and ok(n - 3):
                     stage_q(n - 3)
@@ -346,7 +353,7 @@ def tile_dft_kernel(tc, x_bytes, x_scale, dft_real, dft_imag, out):
                 stage_g(n)
             if ok(n - 4):
                 stage_s(n - 4)
-            if ok(n - 5):
-                stage_l(n - 5)
             if ok(n - 5 - AD):
                 stage_o(n - 5 - AD)
+            if ok(n - 5):
+                stage_l(n - 5)

from contextlib import ExitStack

import concourse.mybir as mybir
from concourse.masks import make_identity

B, K, N = 16384, 512, 256
FLOPS = 2 * B * K * 2 * N

F32 = mybir.dt.float32
BF16 = mybir.dt.bfloat16
U32 = mybir.dt.uint32
U8 = mybir.dt.uint8
FP8 = mybir.dt.float8_e4m3fn
FP8X4 = mybir.dt.float8_e4m3fn_x4
ACT = mybir.ActivationFunctionType
ALU = mybir.AluOpType

P = 128
SUB = 4
NCH = B // (P * SUB)
W2 = 2 * N
CW = 2048
NV = 0
NVF = lambda i: NV
ORD = "caqp"
AD = 1
SPLIT = True
FD = 0
HALFLOAD = 2
PRO, WB, TA, VH, VX, VS = 0, False, 2, 8, 512, 3
RS = lambda i: 1+i%2
RS2 = lambda i: 1
ND, WP, T0F, SQV, LATE, QW = 6, True, 0, 4, 99, 3


HEAD = [[2, 2], [2, 2]]
TAIL = [[2, 2]]


def unit_list():
    sizes = HEAD + [[4]] * (NCH - len(HEAD) - len(TAIL)) + TAIL
    units = []
    for c, parts in enumerate(sizes):
        j0 = 0
        for nj in parts:
            units.append((c, j0, nj))
            j0 += nj
    return units


def direct(i):
    return FD <= i < ND


def resident(i, nj):
    return RS(i) if nj == 4 else RS2(i)


def spot(q, j, ws):
    if ws == 3 and j == 2:
        return 8 * P + q * P
    width = min(ws, 4) if ws != 3 else 2
    return (q * width + j) * P


def tile_dft_kernel(tc, x_bytes, x_scale, dft_real, dft_imag, out):
    nc = tc.nc
    units = unit_list()
    nu = len(units)
    xv = x_bytes.rearrange("(c p j) k -> c p j k", p=P, j=SUB)
    ov = out.rearrange("(c p j) n -> c p j n", p=P, j=SUB)

    with ExitStack() as ctx:
        const = ctx.enter_context(tc.tile_pool(name="const", bufs=1))
        bpool = ctx.enter_context(tc.tile_pool(name="bpool", bufs=NCH))
        work = ctx.enter_context(tc.tile_pool(name="work", bufs=4))
        ring = ctx.enter_context(tc.tile_pool(name="ring", bufs=1))
        outp = ctx.enter_context(tc.tile_pool(name="outp", bufs=8))
        px = ctx.enter_context(tc.psum_pool(name="px", bufs=2))
        pm = ctx.enter_context(tc.psum_pool(name="pm", bufs=4))
        po = ctx.enter_context(tc.psum_pool(name="po", bufs=2))
        ctx.enter_context(tc.manual_schedule())

        s4 = const.tile([P, 4], F32, name="s4")
        nc.sync.dma_start(out=s4[:], in_=x_scale.rearrange("o (p t) -> p (o t)", t=4))
        sc = const.tile([P, K], F32, name="sc")
        wr = const.tile([P, 4 * K], BF16, name="wr")
        xb = []
        for c in range(NCH):
            xbytes = bpool.tile([P, SUB * K], U8, name="xbytes", tag="xbytes")
            step = HALFLOAD if c == 0 else SUB
            for j in range(0, SUB, step):
                nc.sync.dma_start(
                    out=xbytes[:, j * K : (j + step) * K].rearrange("p (j k) -> p j k", j=step),
                    in_=xv[c][:, j : j + step, :],
                )
            xb.append(xbytes)
            if c == 0:
                nc.sync.dma_start(
                    out=wr[:, 0 : 2 * K].rearrange("p (b k) -> p b k", b=2),
                    in_=dft_real.rearrange("(b p) k -> p b k", p=P),
                )
                nc.sync.dma_start(
                    out=wr[:, 2 * K : 4 * K].rearrange("p (b k) -> p b k", b=2),
                    in_=dft_imag.rearrange("(b p) k -> p b k", p=P),
                )

        ident = const.tile([P, P], F32, name="ident")
        make_identity(nc, ident[:])
        one = const.tile([P, 1], F32, name="one")
        nc.vector.memset(one[:], 1.0)
        warm = const.tile([P, 1], F32, name="warm")
        nc.scalar.activation(out=warm[:], in_=one[:], func=ACT.Ln)

        wc = const.tile([P, W2], U32, name="wc", align_bytes=64)
        wsc = const.tile([P, W2], U8, name="wsc", align_bytes=64)

        st = {}

        def transposes(key, src, nj):
            banks = []
            for h in range((nj + 1) // 2):
                if key == "w" and WP:
                    xt = po.tile([P, 2, 2 * P], F32, name="xt", tag="ob")
                else:
                    xt = px.tile([P, 2, 2 * P], F32, name="xt", tag="xt")
                for jj in range(min(2, nj - 2 * h)):
                    j = 2 * h + jj
                    for w in range(2):
                        cols = src[j].bitcast(F32)[:, w : 256 : 2]
                        nc.tensor.transpose(xt[:, w, jj * P : (jj + 1) * P], cols, ident[:])
                banks.append(xt)
            st[("xt", key)] = banks

        def copy_out(key, nj, scaled):
            slot = 4 if key == "w" else key % 4
            gx = ring.tile([P, SUB * K], BF16, name="gx", tag="ring%d" % slot, align_bytes=64)
            gw = gx[:].bitcast(F32)
            for h, xt in enumerate(st[("xt", key)]):
                rows = min(2, nj - 2 * h) * P
                if scaled:
                    nc.vector.tensor_tensor(
                        out=gx[:, 1024 * h : 1024 * h + 4 * rows].rearrange("p (r w e) -> p r w e", w=2, e=2),
                        in0=xt[:].bitcast(BF16)[:, :, 0 : 2 * rows].rearrange("p w (r e) -> p r w e", e=2),
                        in1=s4[:].unsqueeze(1).to_broadcast([P, rows, 4]).rearrange("p r (w e) -> p r w e", w=2),
                        op=ALU.mult,
                    )
                else:
                    nc.scalar.copy(
                        out=gw[:, 512 * h : 512 * h + 2 * rows].rearrange("p (r w) -> p r w", w=2),
                        in_=xt[:, :, 0:rows].rearrange("p w r -> p r w"),
                    )
            st[("gx", key)] = gx

        def quantize(key, nj, codes, scales):
            nc.vector.quantize_mx(out=codes.bitcast(FP8X4), scales=scales, in_=st[("gx", key)][:, 0 : 4 * nj * P])

        def stage_p(i):
            c, j0, nj = units[i]
            if i < VH:
                xs = work.tile([P, SUB * K], BF16, name="xsd", tag="xsd", bufs=3)
                for j in range(nj):
                    piece = xb[c][:, (j0 + j) * K : (j0 + j + 1) * K].bitcast(FP8)
                    if direct(i):
                        nc.vector.tensor_tensor(out=xs[:, j * K : (j + 1) * K], in0=piece, in1=sc[:], op=ALU.mult)
                    elif j == 0:
                        nc.vector.tensor_copy(out=xs[:, 0 : nj * K], in_=xb[c][:, j0 * K : (j0 + nj) * K].bitcast(FP8))
                st[("xs", i)] = [xs[:, j * K : (j + 1) * K] for j in range(nj)]
            else:
                xs = work.tile([P, NV * K], BF16, name="xsv", tag="xsv")
                nv = NVF(i) if nj == 4 else 0
                if nv > 0:
                    nc.vector.tensor_copy(out=xs[:, 0 : nv * K], in_=xb[c][:, j0 * K : (j0 + nv) * K].bitcast(FP8))
                st[("xs", i)] = [xs[:, j * K : (j + 1) * K] for j in range(nv)]

        def stage_g(i):
            c, j0, nj = units[i]
            nv = NVF(i) if nj == 4 else 0
            if i >= VH:
                xs = ring.tile([P, SUB * K], BF16, name="xs", tag="squares%d" % ((i + 2) % 4), align_bytes=64)
                for col in range(nv * K, nj * K, CW):
                    end = min(col + CW, nj * K)
                    nc.gpsimd.tensor_copy(out=xs[:, col:end], in_=xb[c][:, j0 * K + col : j0 * K + end].bitcast(FP8))
                st[("xs", i)] += [xs[:, j * K : (j + 1) * K] for j in range(nv, nj)]

        def stage_t(i):
            transposes(i, st[("xs", i)], units[i][2])

        def stage_c(i):
            copy_out(i, units[i][2], not direct(i))

        def stage_q(i):
            nj = units[i][2]
            xc = work.tile([P, nj * P], U32, name="xc", tag="xc", align_bytes=64)
            xsc = work.tile([P, nj * P], U8, name="xsc", tag="xsc", align_bytes=64)
            quantize(i, nj, xc[:], xsc[:])
            st[("xc", i)] = (xc, xsc)

        wblock = [0, 2, 1, 3]

        def stage_m(i):
            nj = units[i][2]
            xc, xsc = st[("xc", i)]
            rs = resident(i, nj)
            ws = nj - rs
            runs = {4: [(0, 4)], 3: [(0, 2), (2, 1)], 2: [(0, 2)], 1: [(0, 1)], 0: []}[ws]
            banks = []
            for j, nw in runs:
                for q in range(4):
                    col = spot(q, j, ws)
                    if col % W2 == 0:
                        ps = pm.tile([P, W2], F32, name="ps", tag="ps")
                        banks.append(ps)
                    wb = wblock[q]
                    nc.tensor.matmul_mx(
                        out=banks[-1][:, col % W2 : col % W2 + nw * P],
                        lhsT=wc[:, wb * P : (wb + 1) * P].bitcast(FP8X4),
                        lhsT_scale=wsc[:, wb * P : (wb + 1) * P],
                        rhs=xc[:, j * P : (j + nw) * P].bitcast(FP8X4),
                        rhs_scale=xsc[:, j * P : (j + nw) * P],
                        start=True,
                        stop=True,
                    )
            for j in range(ws, nj):
                ps = pm.tile([P, W2], F32, name="ps", tag="ps")
                banks.append(ps)
                nc.tensor.matmul_mx(
                    out=ps[:],
                    lhsT=xc[:, j * P : (j + 1) * P].bitcast(FP8X4),
                    lhsT_scale=xsc[:, j * P : (j + 1) * P],
                    rhs=wc[:].bitcast(FP8X4),
                    rhs_scale=wsc[:],
                    start=True,
                    stop=True,
                )
            st[("ps", i)] = banks

        def stage_s(i):
            nj = units[i][2]
            sq = ring.tile([P, nj * W2], F32, name="sq", tag="squares%d" % (i % 4), align_bytes=64)
            for j, ps in enumerate(st[("ps", i)]):
                dst = sq[:, j * W2 : (j + 1) * W2]
                if i >= nu - SQV and j == len(st[("ps", i)]) - 1:
                    cp = work.tile([P, W2], F32, name="cp", tag="cp")
                    nc.vector.tensor_copy(out=cp[:], in_=ps[:])
                    if SPLIT:
                        if ok(i - 1):
                            stage_a(i - 1)
                    nc.vector.tensor_tensor(out=dst, in0=ps[:], in1=cp[:], op=ALU.mult)
                else:
                    nc.scalar.activation(out=dst, in_=ps[:], func=ACT.Square)
            st[("sq", i)] = sq

        def stage_b(i):
            nj = units[i][2]
            sq = st[("sq", i)]
            ws = nj - resident(i, nj)
            banks = []
            for j in range(ws):
                if j % 2 == 0:
                    ob = po.tile([P, W2], F32, name="ob", tag="ob")
                    banks.append(ob)
                for cb in range(2):
                    dst = banks[-1][:, (j % 2) * N + cb * P : (j % 2) * N + (cb + 1) * P]
                    for part in range(2):
                        col = spot(2 * cb + part, j, ws)
                        nc.tensor.matmul(
                            out=dst,
                            lhsT=sq[:, col : col + P],
                            rhs=ident[:],
                            is_transpose=True,
                            start=(part == 0),
                            stop=(part == 1),
                        )
            st[("ob", i)] = banks

        def stage_a(i):
            nj = units[i][2]
            rs = resident(i, nj)
            if rs > 0:
                sm = work.tile([P, rs * N], F32, name="sm", tag="sm")
                sqv = st[("sq", i)][:, (nj - rs) * W2 : nj * W2].rearrange("p (j c n) -> p j c n", j=rs, c=2)
                nc.vector.tensor_tensor(
                    out=sm[:].rearrange("p (j n) -> p j n", j=rs),
                    in0=sqv[:, :, 0, :],
                    in1=sqv[:, :, 1, :],
                    op=ALU.add,
                )
                st[("sm", i)] = sm

        def stage_l(i):
            c, j0, nj = units[i]
            ot = outp.tile([P, nj * N], F32, name="ot", tag="ot")
            rs = resident(i, nj)
            ws = nj - rs
            for h, ob in enumerate(st[("ob", i)]):
                width = min(2, ws - 2 * h) * N
                nc.scalar.activation(out=ot[:, h * W2 : h * W2 + width], in_=ob[:, 0:width], func=ACT.Ln)
            st[("ot", i)] = ot

        def stage_o(i):
            c, j0, nj = units[i]
            ot = st[("ot", i)]
            rs = resident(i, nj)
            ws = nj - rs
            if rs > 0:
                nc.scalar.activation(out=ot[:, ws * N : nj * N], in_=st[("sm", i)][:], func=ACT.Ln)
            nc.sync.dma_start(out=ov[c][:, j0 : j0 + nj, :], in_=ot[:].rearrange("p (j n) -> p j n", j=nj))

        def ok(i):
            return 0 <= i < nu

        if T0F:
            stage_p(0)
        spread = po.tile([P, 4, P], F32, name="spread", tag="ob")
        for t in range(4):
            nc.tensor.transpose(spread[:, t, :], s4[:, t : t + 1].to_broadcast([P, P]), ident[:])
        nc.scalar.copy(
            out=sc[:].rearrange("p (n t) -> p n t", t=4),
            in_=spread[:].rearrange("p t n -> p n t"),
        )
        for i in range(PRO):
            stage_p(i)
        for i in range(T0F):
            stage_t(i)
        transposes("w", [wr[:, j * K : (j + 1) * K] for j in range(4)], 4)
        copy_out("w", 4, False)

        def vector_turn(n):
            for step in ORD:
                if step == "c" and ok(n) and n >= T0F:
                    stage_p(n)
                if step == "q" and ok(n - 3):
                    stage_q(n - 3)
                if step == "q" and n == QW:
                    quantize("w", 4, wc[:], wsc[:])
                if step == "g" and ok(n):
                    stage_g(n)
                if step == "a" and ok(n - 5 - AD) and not (SPLIT and n - 5 - AD >= nu - SQV - 1 and n - 5 - AD < nu - 1):
                    stage_a(n - 5 - AD)
                if step == "p" and ok(n - 2):
                    stage_c(n - 2)

        for n in range(nu + 5 + AD):
            vector_turn(n)
            if ok(n - 4):
                stage_m(n - 4)
            if ok(n - 5):
                stage_b(n - 5)
            if ok(n - 1) and n - 1 >= T0F:
                stage_t(n - 1)
            if ok(n) and "g" not in ORD:
                stage_g(n)
            if ok(n - 4):
                stage_s(n - 4)
            if ok(n - 5 - AD):
                stage_o(n - 5 - AD)
            if ok(n - 5):
                stage_l(n - 5)
